import numpy as np
import ml_dtypes


def mxq(x, axis, fmt="e4m3"):
    dtype, down = {"e4m3": (ml_dtypes.float8_e4m3fn, 7), "e5m2": (ml_dtypes.float8_e5m2, 14)}[fmt]
    v = np.moveaxis(np.asarray(x, np.float32).astype(ml_dtypes.bfloat16).astype(np.float64), axis, -1)
    blocks = v.reshape(v.shape[:-1] + (-1, 32))
    amax = np.abs(blocks).max(-1, keepdims=True)
    byte = np.maximum(np.where(amax > 0, np.frexp(amax)[1] - 1 + 127, 0) - down, 1)
    scale = np.exp2(byte - 127.0)
    codes = (blocks / scale).astype(np.float32).astype(dtype).astype(np.float64)
    return np.moveaxis((codes * scale).reshape(v.shape), -1, axis)


WIDE = False


def mx_kscale(k):
    if not WIDE:
        return np.ones(k)
    levels = np.array([10, -10, 5, -5, 0])
    if k % 512:
        return np.exp2(np.random.permutation(np.resize(levels, k // 32))).repeat(32)
    a = np.empty((k // 512, 16))
    for p in range(k // 512):
        a[p, :8] = np.random.permutation(np.resize(levels, 8))
        for g in range(8):
            far = levels[np.abs(levels - a[p, g]) >= 10]
            a[p, g + 8] = far[np.random.randint(len(far))]
    return np.exp2(a.ravel()).repeat(32)


BF16 = ml_dtypes.bfloat16


def bf(x):
    return np.asarray(x, np.float32).astype(BF16)


def f64(x):
    return np.asarray(x).astype(np.float64)


B, M, H_ENC, N, H_DEC = 8192, 512, 512, 128, 128
SNR = 25.0
NOISE_STD = float(np.sqrt(1.0 / (2.0 * 10.0 ** (SNR / 10.0))))


def draw0():
    s = mx_kscale(M)
    t = mx_kscale(H_ENC)
    theta = np.random.uniform(0.3, 1.2)
    return {"x": bf(np.random.standard_normal((B, M)) * s),
            "noise": bf(np.random.standard_normal((B, N)) * NOISE_STD),
            "h": bf(np.array([np.cos(theta), np.sin(theta)])),
            "W1": bf(np.random.standard_normal((H_ENC, M)) / np.sqrt(M) / s[None, :] * t[:, None]),
            "b1": bf(np.random.standard_normal(H_ENC) * 0.3 * t),
            "W2": bf(np.random.standard_normal((N, H_ENC)) / np.sqrt(H_ENC) / t[None, :]),
            "b2": bf(np.random.standard_normal(N) * 0.3)}


def core(x, noise, h, W1, b1, W2, b2):
    h = f64(h)
    a = np.maximum((mxq(f64(x), 1, "e4m3") @ mxq(f64(W1), 1, "e4m3").T) + f64(b1), 0.0)
    z = (mxq(a, 1, "e4m3") @ mxq(f64(W2), 1, "e4m3").T) + f64(b2)
    scale = np.sqrt(N * 0.5)
    z = scale * z / np.linalg.norm(z, axis=1, keepdims=True)
    zc = z.reshape(B, N // 2, 2)
    yr = zc[..., 0] * h[0] - zc[..., 1] * h[1]
    yi = zc[..., 0] * h[1] + zc[..., 1] * h[0]
    y = np.stack([yr, yi], axis=-1).reshape(B, N)
    return y + f64(noise)


def e4m3fn_bytes(y):
    return np.clip(np.asarray(y, np.float64), -448.0, 448.0).astype(np.float32).astype(ml_dtypes.float8_e4m3fn).view(np.uint8)


def e4m3fn_values(b):
    return np.asarray(b, np.uint8).view(ml_dtypes.float8_e4m3fn).astype(np.float64)


def setup_inputs():
    d = draw0()
    x0 = np.asarray(d['x']).astype(np.float64)
    s = (np.max(np.abs(x0), axis=(0,), keepdims=True) / 448.0).astype(np.float32)
    out = {}
    for k, v in d.items():
        if k == 'x':
            out['x_bytes'] = e4m3fn_bytes(x0 / s.astype(np.float64))
            out['x_scale'] = s
        else:
            out[k] = v
    return out


def reference(x_bytes, x_scale, noise, h, W1, b1, W2, b2):
    return core(e4m3fn_values(x_bytes) * x_scale.astype(np.float64), noise, h, W1, b1, W2, b2)

@@ -1,0 +1,358 @@
+from contextlib import ExitStack
+
+import concourse.mybir as mybir
+from concourse.masks import make_identity
+
+B, M, H_ENC, N = 8192, 512, 512, 128
+FLOPS = 2 * B * H_ENC * (M + N)
+
+F32 = mybir.dt.float32
+BF16 = mybir.dt.bfloat16
+U32 = mybir.dt.uint32
+U8 = mybir.dt.uint8
+FP8 = mybir.dt.float8_e4m3fn
+FP8X4 = mybir.dt.float8_e4m3fn_x4
+ACT = mybir.ActivationFunctionType
+ALU = mybir.AluOpType
+
+P = 128
+SIZES = [256] + [512] * 15 + [256]
+CHUNKS = len(SIZES)
+INTER_SPLIT = {512: [("V", 0, 448), ("S", 448, 512)], 256: [("V", 0, 224), ("S", 224, 256)]}
+V_RELU = set()
+FAST_INTER = False
+STEPS = [
+    ("quant1", 1),
+    ("cast", 0),
+    ("relu", 2, 1),
+    ("relu", 2, 2),
+    ("transp", 0, 0),
+    ("sumsq", 4, 0),
+    ("sumsq", 4, 1),
+    ("inter", 2, 0),
+    ("inter", 2, 1),
+    ("rnorm", 4),
+    ("final", 4, 0),
+    ("mm2", 3),
+    ("mm1", 1, 0),
+    ("final", 4, 1),
+    ("mm1", 1, 3),
+    ("zbias", 3),
+    ("transp", 0, 1),
+    ("mm1", 1, 1),
+    ("relu", 1, 0),
+    ("evac", 0, 0),
+    ("mm1", 1, 2),
+    ("evac", 0, 1),
+    ("relu", 1, 3),
+    ("rotate", 3),
+    ("quant2", 2),
+]
+
+
+def tile_channel_net_pa_kernel(tc, x_bytes, x_scale, noise, h, W1, b1, W2, b2, out):
+    nc = tc.nc
+    with ExitStack() as ctx:
+        keep = ctx.enter_context(tc.tile_pool(name="keep", bufs=1))
+        work = ctx.enter_context(tc.tile_pool(name="work", bufs=3))
+        ps_x = ctx.enter_context(tc.psum_pool(name="ps_x", bufs=1))
+        ps_a = ctx.enter_context(tc.psum_pool(name="ps_a", bufs=1))
+        ctx.enter_context(tc.manual_schedule())
+
+        starts = [sum(SIZES[:c]) for c in range(CHUNKS)]
+
+        def rows(dram, c):
+            return dram[starts[c] : starts[c] + SIZES[c], :].rearrange("(r j) k -> r (j k)", r=P)
+
+        xb = [keep.tile([P, SIZES[c] // P * M], U8, name=f"xb{c}") for c in range(CHUNKS)]
+        nt = [keep.tile([P, SIZES[c]], BF16, name=f"nt{c}") for c in range(CHUNKS)]
+
+        def load_x(c):
+            nc.sync.dma_start(out=xb[c][:], in_=rows(x_bytes, c))
+
+        def load_noise(c):
+            nc.sync.dma_start(out=nt[c][:], in_=rows(noise, c))
+
+        w1_raw = keep.tile([P, 4, M], BF16, name="w1_raw")
+        w2_raw = keep.tile([P, H_ENC], BF16, name="w2_raw")
+        sc = keep.tile([P, 4], F32, name="sc")
+        b1_raw = keep.tile([P, 4], BF16, name="b1_raw")
+        b2_raw = keep.tile([P, 1], BF16, name="b2_raw")
+        h_raw = keep.tile([P, 2], BF16, name="h_raw")
+        load_x(0)
+        nc.sync.dma_start(out=w1_raw[:], in_=W1.rearrange("(m t) k -> m t k", t=4))
+        nc.sync.dma_start(out=sc[:], in_=x_scale.rearrange("o (p t) -> p (o t)", t=4))
+        nc.sync.dma_start(out=b1_raw[:], in_=b1.rearrange("(p t) -> p t", t=4))
+        load_x(1)
+        nc.sync.dma_start(out=w2_raw[:], in_=W2)
+        nc.sync.dma_start(out=b2_raw[:], in_=b2.rearrange("(p o) -> p o", o=1))
+        nc.sync.dma_start(out=h_raw[:], in_=h.partition_broadcast(P))
+        load_x(2)
+        load_x(3)
+        for c in range(4, CHUNKS):
+            load_x(c)
+            load_noise(c - 4)
+        for c in range(CHUNKS - 4, CHUNKS):
+            load_noise(c)
+
+        ident = keep.tile([P, P], F32, name="ident")
+        make_identity(nc, ident[:])
+        warm = keep.tile([P, 1], F32, name="warm")
+        warm_out = keep.tile([P, 1], F32, name="warm_out")
+        nc.vector.memset(warm[:], 1.0)
+        nc.scalar.activation(out=warm_out[:], in_=warm[:], func=ACT.Abs_reciprocal_sqrt)
+
+        b1f = keep.tile([P, 4], F32, name="b1f")
+        b2f = keep.tile([P, 1], F32, name="b2f")
+        rot_m = keep.tile([P, P], F32, name="rot_m")
+        norm_c = keep.tile([P, 1], F32, name="norm_c")
+
+        def small_constants():
+            nc.gpsimd.tensor_copy(out=b1f[:], in_=b1_raw[:])
+            nc.gpsimd.tensor_copy(out=b2f[:], in_=b2_raw[:])
+
+        hf = keep.tile([P, 2], F32, name="hf")
+        hsq = keep.tile([P, 2], F32, name="hsq")
+        hs = keep.tile([P, 1], F32, name="hs")
+        ind = keep.tile([P, 1], F32, name="ind")
+        hr = keep.tile([P, 1], F32, name="hr")
+        nh1 = keep.tile([P, 1], F32, name="nh1")
+        hn = keep.tile([P, 1], F32, name="hn")
+        rtmp = keep.tile([P, 2, P // 2], F32, name="rtmp")
+
+        def rotation_constants():
+            nc.gpsimd.tensor_copy(out=hf[:], in_=h_raw[:])
+            nc.gpsimd.tensor_tensor(out=hsq[:], in0=hf[:], in1=hf[:], op=ALU.mult)
+            nc.gpsimd.tensor_tensor(out=hs[:], in0=hsq[:, 0:1], in1=hsq[:, 1:2], op=ALU.add)
+            nc.gpsimd.tensor_scalar(out=ind[:], in0=hs[:], scalar1=0.0, scalar2=None, op0=ALU.is_equal)
+            nc.gpsimd.tensor_tensor(out=hr[:], in0=hf[:, 0:1], in1=ind[:], op=ALU.add)
+            nc.gpsimd.tensor_scalar(out=nh1[:], in0=hf[:, 1:2], scalar1=-1.0, scalar2=None, op0=ALU.mult)
+            nc.gpsimd.tensor_tensor(out=hn[:], in0=hs[:], in1=ind[:], op=ALU.add)
+            nc.gpsimd.tensor_scalar(out=hn[:], in0=hn[:], scalar1=64.0, scalar2=None, op0=ALU.mult)
+            nc.vector.reciprocal(out=hn[:], in_=hn[:])
+            nc.gpsimd.tensor_scalar(out=ind[:], in0=ind[:], scalar1=1e30, scalar2=None, op0=ALU.mult)
+            nc.gpsimd.tensor_tensor(out=norm_c[:], in0=hn[:], in1=ind[:], op=ALU.add)
+            iv = ident[:].rearrange("p (j e) -> p e j", e=2)
+            rv = rot_m[:].rearrange("p (j e) -> p e j", e=2)
+            nc.gpsimd.tensor_scalar(out=rtmp[:, 0, :], in0=iv[:, 1, :], scalar1=nh1[:, 0:1], scalar2=None, op0=ALU.mult)
+            nc.gpsimd.tensor_scalar(out=rtmp[:, 1, :], in0=iv[:, 0, :], scalar1=hf[:, 1:2], scalar2=None, op0=ALU.mult)
+            for e in range(2):
+                nc.gpsimd.tensor_scalar(out=rv[:, e, :], in0=iv[:, e, :], scalar1=hr[:, 0:1], scalar2=None, op0=ALU.mult)
+                nc.gpsimd.tensor_tensor(out=rv[:, e, :], in0=rv[:, e, :], in1=rtmp[:, e, :], op=ALU.add)
+
+        w1_codes = keep.tile([P, H_ENC], U32, name="w1_codes", align_bytes=64)
+        w1_scales = keep.tile([P, H_ENC], U8, name="w1_scales", align_bytes=64)
+        w2_codes = keep.tile([P, N], U32, name="w2_codes", align_bytes=64)
+        w2_scales = keep.tile([P, N], U8, name="w2_scales", align_bytes=64)
+        w1g = keep.tile([P, H_ENC, 4], BF16, name="w1g", align_bytes=64)
+        w2g = keep.tile([P, N, 4], BF16, name="w2g", align_bytes=64)
+
+        def w1_transpose(half):
+            words = w1_raw[:].rearrange("p t k -> p (t k)").bitcast(F32)
+            pt = ps_x.tile([P, 2, 256], F32, name=f"xt{half}")
+            for s in range(2):
+                t = 2 * half + s
+                for u in range(2):
+                    nc.tensor.transpose(
+                        pt[:, u, s * P : (s + 1) * P], words[:, t * 256 + u : (t + 1) * 256 : 2], ident[:]
+                    )
+            wv = w1g[:].rearrange("p c t -> p (c t)")[:, half * 1024 : (half + 1) * 1024].bitcast(F32)
+            nc.vector.tensor_copy(out=wv.rearrange("p (r u) -> p r u", u=2), in_=pt[:].rearrange("p u r -> p r u"))
+
+        def w1_quant():
+            nc.vector.quantize_mx(
+                out=w1_codes[:].bitcast(FP8X4), scales=w1_scales[:], in_=w1g[:].rearrange("p c t -> p (c t)")
+            )
+
+        def w2_prepare():
+            words = w2_raw[:].bitcast(F32)
+            pt = ps_a.tile([P, 2, P], F32, name="z")
+            for u in range(2):
+                nc.tensor.transpose(pt[:, u, :], words[:, u : 256 : 2], ident[:])
+            wv = w2g[:].rearrange("p c t -> p (c t)").bitcast(F32)
+            nc.vector.tensor_copy(out=wv.rearrange("p (r u) -> p r u", u=2), in_=pt[:].rearrange("p u r -> p r u"))
+
+        def w2_quant():
+            nc.vector.quantize_mx(
+                out=w2_codes[:].bitcast(FP8X4), scales=w2_scales[:], in_=w2g[:].rearrange("p c t -> p (c t)")
+            )
+
+        T = {}
+        scv = sc[:].rearrange("p (u e) -> p u e", u=2).unsqueeze(1).broadcast_to([P, 256, 2, 2])
+
+        def cast(c):
+            n = SIZES[c]
+            xs = work.tile([P, n * 4], BF16, name="xs")
+            T["xs", c] = xs
+            for eng, lo, hi in [("S", 0, n * 4)]:
+                if eng == "S":
+                    nc.scalar.copy(out=xs[:, lo:hi], in_=xb[c][:, lo:hi].bitcast(FP8))
+                else:
+                    nc.vector.tensor_copy(out=xs[:, lo:hi], in_=xb[c][:, lo:hi].bitcast(FP8))
+
+        def transp(c, half):
+            if half * 256 >= SIZES[c]:
+                return
+            words = T["xs", c][:].bitcast(F32)
+            pt = ps_x.tile([P, 2, 256], F32, name=f"xt{(half + c) % 2}")
+            T["xt", c, half] = pt
+            for s in range(2):
+                j = 2 * half + s
+                for u in range(2):
+                    nc.tensor.transpose(
+                        pt[:, u, s * P : (s + 1) * P], words[:, j * 256 + u : (j + 1) * 256 : 2], ident[:]
+                    )
+
+        def evac(c, half):
+            if half * 256 >= SIZES[c]:
+                return
+            if half == 0:
+                xg = work.tile([P, SIZES[c], 4], BF16, name="xg", align_bytes=64)
+                T["xg", c] = xg
+            xg = T["xg", c]
+            pv = T["xt", c, half][:].rearrange("p u r -> p (u r)").bitcast(BF16)
+            nc.vector.tensor_tensor(
+                out=xg[:, half * 256 : (half + 1) * 256, :].rearrange("p r (u e) -> p r u e", u=2),
+                in0=pv.rearrange("p (u r e) -> p r u e", u=2, e=2),
+                in1=scv,
+                op=ALU.mult,
+            )
+
+        def quant1(c):
+            xc = work.tile([P, SIZES[c]], U32, name="xc", align_bytes=64)
+            xsc = work.tile([P, SIZES[c]], U8, name="xsc", align_bytes=64)
+            T["xc", c] = xc
+            T["xsc", c] = xsc
+            nc.vector.quantize_mx(
+                out=xc[:].bitcast(FP8X4), scales=xsc[:], in_=T["xg", c][:].rearrange("p r t -> p (r t)")
+            )
+
+        def mm1(c, t):
+            pa = ps_a.tile([P, SIZES[c]], F32, name=f"a{t}")
+            T["pa", c, t] = pa
+            nc.tensor.matmul_mx(
+                out=pa[:],
+                lhsT=w1_codes[:, t * P : (t + 1) * P].bitcast(FP8X4),
+                lhsT_scale=w1_scales[:, t * P : (t + 1) * P],
+                rhs=T["xc", c][:].bitcast(FP8X4),
+                rhs_scale=T["xsc", c][:],
+                start=True,
+                stop=True,
+            )
+
+        def relu(c, t):
+            if t == 0:
+                ap = work.tile([P, 4, SIZES[c]], BF16, name="ap", align_bytes=64)
+                T["ap", c] = ap
+            ap = T["ap", c]
+            if (c, t) in V_RELU:
+                nc.vector.tensor_scalar(
+                    out=ap[:, t, :], in0=T["pa", c, t][:], scalar1=b1f[:, t : t + 1], scalar2=0.0,
+                    op0=ALU.add, op1=ALU.max,
+                )
+            else:
+                nc.scalar.activation(out=ap[:, t, :], in_=T["pa", c, t][:], func=ACT.Relu, bias=b1f[:, t : t + 1])
+
+        def inter(c, part):
+            if part == 0:
+                ag = work.tile([P, SIZES[c], 4], BF16, name="ag", align_bytes=64)
+                T["ag", c] = ag
+            ag = T["ag", c]
+            eng, lo, hi = INTER_SPLIT[SIZES[c]][part]
+            o = ag[:, lo:hi, :]
+            a = T["ap", c][:, :, lo:hi].rearrange("p t n -> p n t")
+            if FAST_INTER:
+                o = ag[:, lo:hi, :].rearrange("p (c i) t -> p c t i", i=4)
+                a = T["ap", c][:, :, lo:hi].rearrange("p t (c i) -> p c t i", i=4)
+            if eng == "V":
+                nc.vector.tensor_copy(out=o, in_=a)
+            elif eng == "S":
+                nc.scalar.copy(out=o, in_=a)
+            else:
+                nc.gpsimd.tensor_scalar(out=o, in0=a, scalar1=1.0, scalar2=0.0, op0=ALU.mult, op1=ALU.add)
+
+        def quant2(c):
+            ac = work.tile([P, SIZES[c]], U32, name="ac", align_bytes=64)
+            asc = work.tile([P, SIZES[c]], U8, name="asc", align_bytes=64)
+            T["ac", c] = ac
+            T["asc", c] = asc
+            nc.vector.quantize_mx(
+                out=ac[:].bitcast(FP8X4), scales=asc[:], in_=T["ag", c][:].rearrange("p r t -> p (r t)")
+            )
+
+        def mm2(c):
+            pz = ps_a.tile([P, SIZES[c]], F32, name="z")
+            T["pz", c] = pz
+            nc.tensor.matmul_mx(
+                out=pz[:],
+                lhsT=w2_codes[:].bitcast(FP8X4),
+                lhsT_scale=w2_scales[:],
+                rhs=T["ac", c][:].bitcast(FP8X4),
+                rhs_scale=T["asc", c][:],
+                start=True,
+                stop=True,
+            )
+
+        def zbias(c):
+            zb = work.tile([P, SIZES[c]], F32, name="zb")
+            T["zb", c] = zb
+            nc.scalar.activation(out=zb[:], in_=T["pz", c][:], func=ACT.Identity, bias=b2f[:, 0:1])
+
+        def rotate(c):
+            py = ps_a.tile([P, SIZES[c] // P, N], F32, name="y")
+            T["py", c] = py
+            for j in range(SIZES[c] // P):
+                nc.tensor.matmul(
+                    py[:, j, :], lhsT=T["zb", c][:, j * P : (j + 1) * P], rhs=rot_m[:], start=True, stop=True
+                )
+
+        def sumsq(c, half):
+            if half * 256 >= SIZES[c]:
+                return
+            if half == 0:
+                T["ss", c] = work.tile([P, SIZES[c] // P], F32, name="ss")
+            ss = T["ss", c]
+            for j in (2 * half, 2 * half + 1):
+                junk = work.tile([P, N], BF16, name="junk")
+                nc.scalar.activation(
+                    out=junk[:], in_=T["py", c][:, j, :], func=ACT.Square, accum_out=ss[:, j : j + 1]
+                )
+
+        def rnorm(c):
+            rs = work.tile([P, SIZES[c] // P], F32, name="rs")
+            T["rs", c] = rs
+            nc.scalar.activation(
+                out=rs[:], in_=T["ss", c][:], func=ACT.Abs_reciprocal_sqrt, scale=norm_c[:, 0:1]
+            )
+
+        def final(c, half):
+            if half * 256 >= SIZES[c]:
+                return
+            if half == 0:
+                T["o", c] = work.tile([P, SIZES[c] // P, N], F32, name="o")
+            o = T["o", c]
+            for j in (2 * half, 2 * half + 1):
+                nc.vector.scalar_tensor_tensor(
+                    out=o[:, j, :], in0=T["py", c][:, j, :], scalar=T["rs", c][:, j : j + 1],
+                    in1=nt[c][:, j * N : (j + 1) * N], op0=ALU.mult, op1=ALU.add,
+                )
+            if (half + 1) * 256 == SIZES[c]:
+                nc.sync.dma_start(out=rows(out, c), in_=o[:].rearrange("p j n -> p (j n)"))
+
+
+        small_constants()
+        cast(0)
+        w1_transpose(0)
+        w1_transpose(1)
+        w1_quant()
+        fns = {"cast": cast, "transp": transp, "evac": evac, "quant1": quant1, "mm1": mm1, "relu": relu, "inter": inter,
+               "quant2": quant2, "mm2": mm2, "zbias": zbias, "rotate": rotate, "sumsq": sumsq, "rnorm": rnorm, "final": final}
+        for i in range(CHUNKS + max(st[1] for st in STEPS)):
+            for st in STEPS:
+                c = i - st[1]
+                if 0 <= c < CHUNKS and not (st[0] == "cast" and c == 0):
+                    fns[st[0]](c, *st[2:])
+            if i == 0:
+                w2_prepare()
+                w2_quant()
+                rotation_constants()

@@ -18,35 +18,37 @@ ALU = mybir.AluOpType
 P = 128
 SIZES = [256] + [512] * 15 + [256]
 CHUNKS = len(SIZES)
-INTER_SPLIT = {512: [("V", 0, 448), ("S", 448, 512)], 256: [("V", 0, 224), ("S", 224, 256)]}
-V_RELU = set()
+INTER_SPLIT = {512: [("G", 0, 128), ("G", 128, 256), ("G", 256, 384), ("G", 384, 512)], 256: [("G", 0, 128), ("G", 128, 256)]}
+V_RELU = {(c, 3) for c in range(1, CHUNKS, 3)}
 FAST_INTER = False
 STEPS = [
-    ("quant1", 1),
     ("cast", 0),
-    ("relu", 2, 1),
-    ("relu", 2, 2),
     ("transp", 0, 0),
+    ("relu", 2, 3),
+    ("relu", 2, 2),
+    ("relu", 2, 1),
     ("sumsq", 4, 0),
+    ("mm1", 1, 0),
+    ("quant2", 3),
     ("sumsq", 4, 1),
     ("inter", 2, 0),
-    ("inter", 2, 1),
-    ("rnorm", 4),
-    ("final", 4, 0),
-    ("mm2", 3),
-    ("mm1", 1, 0),
-    ("final", 4, 1),
-    ("mm1", 1, 3),
-    ("zbias", 3),
-    ("transp", 0, 1),
-    ("mm1", 1, 1),
-    ("relu", 1, 0),
     ("evac", 0, 0),
+    ("relu", 1, 0),
+    ("mm2", 3),
+    ("transp", 0, 1),
+    ("rnorm", 4),
+    ("mm1", 1, 3),
+    ("final", 4, 0),
+    ("mm1", 1, 1),
     ("mm1", 1, 2),
+    ("inter", 2, 2),
+    ("zbias", 3),
     ("evac", 0, 1),
-    ("relu", 1, 3),
+    ("inter", 2, 3),
+    ("final", 4, 1),
+    ("inter", 2, 1),
+    ("quant1", 0),
     ("rotate", 3),
-    ("quant2", 2),
 ]
 
 
@@ -254,6 +256,8 @@ def tile_channel_net_pa_kernel(tc, x_bytes, x_scale, noise, h, W1, b1, W2, b2, o
                 nc.scalar.activation(out=ap[:, t, :], in_=T["pa", c, t][:], func=ACT.Relu, bias=b1f[:, t : t + 1])
 
         def inter(c, part):
+            if part >= len(INTER_SPLIT[SIZES[c]]):
+                return
             if part == 0:
                 ag = work.tile([P, SIZES[c], 4], BF16, name="ag", align_bytes=64)
                 T["ag", c] = ag

from contextlib import ExitStack

import concourse.mybir as mybir
from concourse.masks import make_identity

B, M, H_ENC, N = 8192, 512, 512, 128
FLOPS = 2 * B * H_ENC * (M + N)

F32 = mybir.dt.float32
BF16 = mybir.dt.bfloat16
U32 = mybir.dt.uint32
U8 = mybir.dt.uint8
FP8 = mybir.dt.float8_e4m3fn
FP8X4 = mybir.dt.float8_e4m3fn_x4
ACT = mybir.ActivationFunctionType
ALU = mybir.AluOpType

P = 128
SIZES = [256] + [512] * 15 + [256]
CHUNKS = len(SIZES)
INTER_SPLIT = {512: [("G", 0, 128), ("G", 128, 256), ("G", 256, 384), ("G", 384, 512)], 256: [("G", 0, 128), ("G", 128, 256)]}
V_RELU = {(c, 3) for c in range(1, CHUNKS, 3)}
FAST_INTER = False
STEPS = [
    ("cast", 0),
    ("transp", 0, 0),
    ("relu", 2, 3),
    ("relu", 2, 2),
    ("relu", 2, 1),
    ("sumsq", 4, 0),
    ("mm1", 1, 0),
    ("quant2", 3),
    ("sumsq", 4, 1),
    ("inter", 2, 0),
    ("evac", 0, 0),
    ("relu", 1, 0),
    ("mm2", 3),
    ("transp", 0, 1),
    ("rnorm", 4),
    ("mm1", 1, 3),
    ("final", 4, 0),
    ("mm1", 1, 1),
    ("mm1", 1, 2),
    ("inter", 2, 2),
    ("zbias", 3),
    ("evac", 0, 1),
    ("inter", 2, 3),
    ("final", 4, 1),
    ("inter", 2, 1),
    ("quant1", 0),
    ("rotate", 3),
]


def tile_channel_net_pa_kernel(tc, x_bytes, x_scale, noise, h, W1, b1, W2, b2, out):
    nc = tc.nc
    with ExitStack() as ctx:
        keep = ctx.enter_context(tc.tile_pool(name="keep", bufs=1))
        work = ctx.enter_context(tc.tile_pool(name="work", bufs=3))
        ps_x = ctx.enter_context(tc.psum_pool(name="ps_x", bufs=1))
        ps_a = ctx.enter_context(tc.psum_pool(name="ps_a", bufs=1))
        ctx.enter_context(tc.manual_schedule())

        starts = [sum(SIZES[:c]) for c in range(CHUNKS)]

        def rows(dram, c):
            return dram[starts[c] : starts[c] + SIZES[c], :].rearrange("(r j) k -> r (j k)", r=P)

        xb = [keep.tile([P, SIZES[c] // P * M], U8, name=f"xb{c}") for c in range(CHUNKS)]
        nt = [keep.tile([P, SIZES[c]], BF16, name=f"nt{c}") for c in range(CHUNKS)]

        def load_x(c):
            nc.sync.dma_start(out=xb[c][:], in_=rows(x_bytes, c))

        def load_noise(c):
            nc.sync.dma_start(out=nt[c][:], in_=rows(noise, c))

        w1_raw = keep.tile([P, 4, M], BF16, name="w1_raw")
        w2_raw = keep.tile([P, H_ENC], BF16, name="w2_raw")
        sc = keep.tile([P, 4], F32, name="sc")
        b1_raw = keep.tile([P, 4], BF16, name="b1_raw")
        b2_raw = keep.tile([P, 1], BF16, name="b2_raw")
        h_raw = keep.tile([P, 2], BF16, name="h_raw")
        load_x(0)
        nc.sync.dma_start(out=w1_raw[:], in_=W1.rearrange("(m t) k -> m t k", t=4))
        nc.sync.dma_start(out=sc[:], in_=x_scale.rearrange("o (p t) -> p (o t)", t=4))
        nc.sync.dma_start(out=b1_raw[:], in_=b1.rearrange("(p t) -> p t", t=4))
        load_x(1)
        nc.sync.dma_start(out=w2_raw[:], in_=W2)
        nc.sync.dma_start(out=b2_raw[:], in_=b2.rearrange("(p o) -> p o", o=1))
        nc.sync.dma_start(out=h_raw[:], in_=h.partition_broadcast(P))
        load_x(2)
        load_x(3)
        for c in range(4, CHUNKS):
            load_x(c)
            load_noise(c - 4)
        for c in range(CHUNKS - 4, CHUNKS):
            load_noise(c)

        ident = keep.tile([P, P], F32, name="ident")
        make_identity(nc, ident[:])
        warm = keep.tile([P, 1], F32, name="warm")
        warm_out = keep.tile([P, 1], F32, name="warm_out")
        nc.vector.memset(warm[:], 1.0)
        nc.scalar.activation(out=warm_out[:], in_=warm[:], func=ACT.Abs_reciprocal_sqrt)

        b1f = keep.tile([P, 4], F32, name="b1f")
        b2f = keep.tile([P, 1], F32, name="b2f")
        rot_m = keep.tile([P, P], F32, name="rot_m")
        norm_c = keep.tile([P, 1], F32, name="norm_c")

        def small_constants():
            nc.gpsimd.tensor_copy(out=b1f[:], in_=b1_raw[:])
            nc.gpsimd.tensor_copy(out=b2f[:], in_=b2_raw[:])

        hf = keep.tile([P, 2], F32, name="hf")
        hsq = keep.tile([P, 2], F32, name="hsq")
        hs = keep.tile([P, 1], F32, name="hs")
        ind = keep.tile([P, 1], F32, name="ind")
        hr = keep.tile([P, 1], F32, name="hr")
        nh1 = keep.tile([P, 1], F32, name="nh1")
        hn = keep.tile([P, 1], F32, name="hn")
        rtmp = keep.tile([P, 2, P // 2], F32, name="rtmp")

        def rotation_constants():
            nc.gpsimd.tensor_copy(out=hf[:], in_=h_raw[:])
            nc.gpsimd.tensor_tensor(out=hsq[:], in0=hf[:], in1=hf[:], op=ALU.mult)
            nc.gpsimd.tensor_tensor(out=hs[:], in0=hsq[:, 0:1], in1=hsq[:, 1:2], op=ALU.add)
            nc.gpsimd.tensor_scalar(out=ind[:], in0=hs[:], scalar1=0.0, scalar2=None, op0=ALU.is_equal)
            nc.gpsimd.tensor_tensor(out=hr[:], in0=hf[:, 0:1], in1=ind[:], op=ALU.add)
            nc.gpsimd.tensor_scalar(out=nh1[:], in0=hf[:, 1:2], scalar1=-1.0, scalar2=None, op0=ALU.mult)
            nc.gpsimd.tensor_tensor(out=hn[:], in0=hs[:], in1=ind[:], op=ALU.add)
            nc.gpsimd.tensor_scalar(out=hn[:], in0=hn[:], scalar1=64.0, scalar2=None, op0=ALU.mult)
            nc.vector.reciprocal(out=hn[:], in_=hn[:])
            nc.gpsimd.tensor_scalar(out=ind[:], in0=ind[:], scalar1=1e30, scalar2=None, op0=ALU.mult)
            nc.gpsimd.tensor_tensor(out=norm_c[:], in0=hn[:], in1=ind[:], op=ALU.add)
            iv = ident[:].rearrange("p (j e) -> p e j", e=2)
            rv = rot_m[:].rearrange("p (j e) -> p e j", e=2)
            nc.gpsimd.tensor_scalar(out=rtmp[:, 0, :], in0=iv[:, 1, :], scalar1=nh1[:, 0:1], scalar2=None, op0=ALU.mult)
            nc.gpsimd.tensor_scalar(out=rtmp[:, 1, :], in0=iv[:, 0, :], scalar1=hf[:, 1:2], scalar2=None, op0=ALU.mult)
            for e in range(2):
                nc.gpsimd.tensor_scalar(out=rv[:, e, :], in0=iv[:, e, :], scalar1=hr[:, 0:1], scalar2=None, op0=ALU.mult)
                nc.gpsimd.tensor_tensor(out=rv[:, e, :], in0=rv[:, e, :], in1=rtmp[:, e, :], op=ALU.add)

        w1_codes = keep.tile([P, H_ENC], U32, name="w1_codes", align_bytes=64)
        w1_scales = keep.tile([P, H_ENC], U8, name="w1_scales", align_bytes=64)
        w2_codes = keep.tile([P, N], U32, name="w2_codes", align_bytes=64)
        w2_scales = keep.tile([P, N], U8, name="w2_scales", align_bytes=64)
        w1g = keep.tile([P, H_ENC, 4], BF16, name="w1g", align_bytes=64)
        w2g = keep.tile([P, N, 4], BF16, name="w2g", align_bytes=64)

        def w1_transpose(half):
            words = w1_raw[:].rearrange("p t k -> p (t k)").bitcast(F32)
            pt = ps_x.tile([P, 2, 256], F32, name=f"xt{half}")
            for s in range(2):
                t = 2 * half + s
                for u in range(2):
                    nc.tensor.transpose(
                        pt[:, u, s * P : (s + 1) * P], words[:, t * 256 + u : (t + 1) * 256 : 2], ident[:]
                    )
            wv = w1g[:].rearrange("p c t -> p (c t)")[:, half * 1024 : (half + 1) * 1024].bitcast(F32)
            nc.vector.tensor_copy(out=wv.rearrange("p (r u) -> p r u", u=2), in_=pt[:].rearrange("p u r -> p r u"))

        def w1_quant():
            nc.vector.quantize_mx(
                out=w1_codes[:].bitcast(FP8X4), scales=w1_scales[:], in_=w1g[:].rearrange("p c t -> p (c t)")
            )

        def w2_prepare():
            words = w2_raw[:].bitcast(F32)
            pt = ps_a.tile([P, 2, P], F32, name="z")
            for u in range(2):
                nc.tensor.transpose(pt[:, u, :], words[:, u : 256 : 2], ident[:])
            wv = w2g[:].rearrange("p c t -> p (c t)").bitcast(F32)
            nc.vector.tensor_copy(out=wv.rearrange("p (r u) -> p r u", u=2), in_=pt[:].rearrange("p u r -> p r u"))

        def w2_quant():
            nc.vector.quantize_mx(
                out=w2_codes[:].bitcast(FP8X4), scales=w2_scales[:], in_=w2g[:].rearrange("p c t -> p (c t)")
            )

        T = {}
        scv = sc[:].rearrange("p (u e) -> p u e", u=2).unsqueeze(1).broadcast_to([P, 256, 2, 2])

        def cast(c):
            n = SIZES[c]
            xs = work.tile([P, n * 4], BF16, name="xs")
            T["xs", c] = xs
            for eng, lo, hi in [("S", 0, n * 4)]:
                if eng == "S":
                    nc.scalar.copy(out=xs[:, lo:hi], in_=xb[c][:, lo:hi].bitcast(FP8))
                else:
                    nc.vector.tensor_copy(out=xs[:, lo:hi], in_=xb[c][:, lo:hi].bitcast(FP8))

        def transp(c, half):
            if half * 256 >= SIZES[c]:
                return
            words = T["xs", c][:].bitcast(F32)
            pt = ps_x.tile([P, 2, 256], F32, name=f"xt{(half + c) % 2}")
            T["xt", c, half] = pt
            for s in range(2):
                j = 2 * half + s
                for u in range(2):
                    nc.tensor.transpose(
                        pt[:, u, s * P : (s + 1) * P], words[:, j * 256 + u : (j + 1) * 256 : 2], ident[:]
                    )

        def evac(c, half):
            if half * 256 >= SIZES[c]:
                return
            if half == 0:
                xg = work.tile([P, SIZES[c], 4], BF16, name="xg", align_bytes=64)
                T["xg", c] = xg
            xg = T["xg", c]
            pv = T["xt", c, half][:].rearrange("p u r -> p (u r)").bitcast(BF16)
            nc.vector.tensor_tensor(
                out=xg[:, half * 256 : (half + 1) * 256, :].rearrange("p r (u e) -> p r u e", u=2),
                in0=pv.rearrange("p (u r e) -> p r u e", u=2, e=2),
                in1=scv,
                op=ALU.mult,
            )

        def quant1(c):
            xc = work.tile([P, SIZES[c]], U32, name="xc", align_bytes=64)
            xsc = work.tile([P, SIZES[c]], U8, name="xsc", align_bytes=64)
            T["xc", c] = xc
            T["xsc", c] = xsc
            nc.vector.quantize_mx(
                out=xc[:].bitcast(FP8X4), scales=xsc[:], in_=T["xg", c][:].rearrange("p r t -> p (r t)")
            )

        def mm1(c, t):
            pa = ps_a.tile([P, SIZES[c]], F32, name=f"a{t}")
            T["pa", c, t] = pa
            nc.tensor.matmul_mx(
                out=pa[:],
                lhsT=w1_codes[:, t * P : (t + 1) * P].bitcast(FP8X4),
                lhsT_scale=w1_scales[:, t * P : (t + 1) * P],
                rhs=T["xc", c][:].bitcast(FP8X4),
                rhs_scale=T["xsc", c][:],
                start=True,
                stop=True,
            )

        def relu(c, t):
            if t == 0:
                ap = work.tile([P, 4, SIZES[c]], BF16, name="ap", align_bytes=64)
                T["ap", c] = ap
            ap = T["ap", c]
            if (c, t) in V_RELU:
                nc.vector.tensor_scalar(
                    out=ap[:, t, :], in0=T["pa", c, t][:], scalar1=b1f[:, t : t + 1], scalar2=0.0,
                    op0=ALU.add, op1=ALU.max,
                )
            else:
                nc.scalar.activation(out=ap[:, t, :], in_=T["pa", c, t][:], func=ACT.Relu, bias=b1f[:, t : t + 1])

        def inter(c, part):
            if part >= len(INTER_SPLIT[SIZES[c]]):
                return
            if part == 0:
                ag = work.tile([P, SIZES[c], 4], BF16, name="ag", align_bytes=64)
                T["ag", c] = ag
            ag = T["ag", c]
            eng, lo, hi = INTER_SPLIT[SIZES[c]][part]
            o = ag[:, lo:hi, :]
            a = T["ap", c][:, :, lo:hi].rearrange("p t n -> p n t")
            if FAST_INTER:
                o = ag[:, lo:hi, :].rearrange("p (c i) t -> p c t i", i=4)
                a = T["ap", c][:, :, lo:hi].rearrange("p t (c i) -> p c t i", i=4)
            if eng == "V":
                nc.vector.tensor_copy(out=o, in_=a)
            elif eng == "S":
                nc.scalar.copy(out=o, in_=a)
            else:
                nc.gpsimd.tensor_scalar(out=o, in0=a, scalar1=1.0, scalar2=0.0, op0=ALU.mult, op1=ALU.add)

        def quant2(c):
            ac = work.tile([P, SIZES[c]], U32, name="ac", align_bytes=64)
            asc = work.tile([P, SIZES[c]], U8, name="asc", align_bytes=64)
            T["ac", c] = ac
            T["asc", c] = asc
            nc.vector.quantize_mx(
                out=ac[:].bitcast(FP8X4), scales=asc[:], in_=T["ag", c][:].rearrange("p r t -> p (r t)")
            )

        def mm2(c):
            pz = ps_a.tile([P, SIZES[c]], F32, name="z")
            T["pz", c] = pz
            nc.tensor.matmul_mx(
                out=pz[:],
                lhsT=w2_codes[:].bitcast(FP8X4),
                lhsT_scale=w2_scales[:],
                rhs=T["ac", c][:].bitcast(FP8X4),
                rhs_scale=T["asc", c][:],
                start=True,
                stop=True,
            )

        def zbias(c):
            zb = work.tile([P, SIZES[c]], F32, name="zb")
            T["zb", c] = zb
            nc.scalar.activation(out=zb[:], in_=T["pz", c][:], func=ACT.Identity, bias=b2f[:, 0:1])

        def rotate(c):
            py = ps_a.tile([P, SIZES[c] // P, N], F32, name="y")
            T["py", c] = py
            for j in range(SIZES[c] // P):
                nc.tensor.matmul(
                    py[:, j, :], lhsT=T["zb", c][:, j * P : (j + 1) * P], rhs=rot_m[:], start=True, stop=True
                )

        def sumsq(c, half):
            if half * 256 >= SIZES[c]:
                return
            if half == 0:
                T["ss", c] = work.tile([P, SIZES[c] // P], F32, name="ss")
            ss = T["ss", c]
            for j in (2 * half, 2 * half + 1):
                junk = work.tile([P, N], BF16, name="junk")
                nc.scalar.activation(
                    out=junk[:], in_=T["py", c][:, j, :], func=ACT.Square, accum_out=ss[:, j : j + 1]
                )

        def rnorm(c):
            rs = work.tile([P, SIZES[c] // P], F32, name="rs")
            T["rs", c] = rs
            nc.scalar.activation(
                out=rs[:], in_=T["ss", c][:], func=ACT.Abs_reciprocal_sqrt, scale=norm_c[:, 0:1]
            )

        def final(c, half):
            if half * 256 >= SIZES[c]:
                return
            if half == 0:
                T["o", c] = work.tile([P, SIZES[c] // P, N], F32, name="o")
            o = T["o", c]
            for j in (2 * half, 2 * half + 1):
                nc.vector.scalar_tensor_tensor(
                    out=o[:, j, :], in0=T["py", c][:, j, :], scalar=T["rs", c][:, j : j + 1],
                    in1=nt[c][:, j * N : (j + 1) * N], op0=ALU.mult, op1=ALU.add,
                )
            if (half + 1) * 256 == SIZES[c]:
                nc.sync.dma_start(out=rows(out, c), in_=o[:].rearrange("p j n -> p (j n)"))


        small_constants()
        cast(0)
        w1_transpose(0)
        w1_transpose(1)
        w1_quant()
        fns = {"cast": cast, "transp": transp, "evac": evac, "quant1": quant1, "mm1": mm1, "relu": relu, "inter": inter,
               "quant2": quant2, "mm2": mm2, "zbias": zbias, "rotate": rotate, "sumsq": sumsq, "rnorm": rnorm, "final": final}
        for i in range(CHUNKS + max(st[1] for st in STEPS)):
            for st in STEPS:
                c = i - st[1]
                if 0 <= c < CHUNKS and not (st[0] == "cast" and c == 0):
                    fns[st[0]](c, *st[2:])
            if i == 0:
                w2_prepare()
                w2_quant()
                rotation_constants()
